import numpy as np
import ml_dtypes


def mxq(x, axis, fmt="e4m3"):
    dtype, down = {"e4m3": (ml_dtypes.float8_e4m3fn, 7), "e5m2": (ml_dtypes.float8_e5m2, 14)}[fmt]
    v = np.moveaxis(np.asarray(x, np.float32).astype(ml_dtypes.bfloat16).astype(np.float64), axis, -1)
    blocks = v.reshape(v.shape[:-1] + (-1, 32))
    amax = np.abs(blocks).max(-1, keepdims=True)
    byte = np.maximum(np.where(amax > 0, np.frexp(amax)[1] - 1 + 127, 0) - down, 1)
    scale = np.exp2(byte - 127.0)
    codes = (blocks / scale).astype(np.float32).astype(dtype).astype(np.float64)
    return np.moveaxis((codes * scale).reshape(v.shape), -1, axis)


WIDE = False


def mx_kscale(k):
    if not WIDE:
        return np.ones(k)
    levels = np.array([10, -10, 5, -5, 0])
    a = np.random.permutation(np.resize(levels, k // 512 * 4)).reshape(k // 512, 4)
    idx = np.arange(k)
    return np.exp2(a[idx // 512, idx % 128 // 32])


BF16 = ml_dtypes.bfloat16


def bf(x):
    return np.asarray(x, np.float32).astype(BF16)


def f64(x):
    return np.asarray(x).astype(np.float64)


B, I, H = 128, 2048, 2048
EPS = 1e-5


def sigmoid(v):
    return 1.0 / (1.0 + np.exp(-v))


def ln(v, g, b):
    m = v.mean(-1, keepdims=True)
    var = np.square(v - m).mean(-1, keepdims=True)
    return (v - m) / np.sqrt(var + EPS) * g + b


def setup_inputs():
    s, t = mx_kscale(I), mx_kscale(H)
    d = {"x": bf(np.random.standard_normal((B, I)) * s), "h": bf(np.random.standard_normal((B, H)) * t)}
    for g in ("i", "c"):
        d["W" + g + "_w"] = bf(np.random.standard_normal((H, I)) / np.sqrt(I) / s[None, :])
        d["W" + g + "_b"] = bf(np.random.standard_normal(H) * 0.5)
        d["U" + g + "_w"] = bf(np.random.standard_normal((H, H)) / np.sqrt(H) / t[None, :])
        d["ln" + g + "_g"] = bf(1.0 + 0.2 * np.random.standard_normal(H))
        d["ln" + g + "_b"] = bf(0.2 * np.random.standard_normal(H))
    return d


def reference(x, h, Wi_w, Wi_b, Ui_w, lni_g, lni_b, Wc_w, Wc_b, Uc_w, lnc_g, lnc_b):
    xq = mxq(f64(x), 1, "e4m3")
    hq = mxq(f64(h), 1, "e4m3")
    pre_i = (xq @ mxq(f64(Wi_w), 1, "e4m3").T) + f64(Wi_b) + (hq @ mxq(f64(Ui_w), 1, "e4m3").T)
    pre_c = (xq @ mxq(f64(Wc_w), 1, "e4m3").T) + f64(Wc_b) + (hq @ mxq(f64(Uc_w), 1, "e4m3").T)
    i = sigmoid(ln(pre_i, f64(lni_g), f64(lni_b)))
    c_tilde = np.tanh(ln(pre_c, f64(lnc_g), f64(lnc_b)))
    return i * c_tilde

@@ -1,0 +1,267 @@
+from contextlib import ExitStack
+
+import concourse.mybir as mybir
+from concourse.masks import make_identity
+
+F32 = mybir.dt.float32
+BF16 = mybir.dt.bfloat16
+U32 = mybir.dt.uint32
+U8 = mybir.dt.uint8
+FP8X4 = mybir.dt.float8_e4m3fn_x4
+ALU = mybir.AluOpType
+ACT = mybir.ActivationFunctionType
+
+P = 128
+FEATURES = 2048
+HIDDEN = 2048
+GATES = 2
+OPERANDS = 2
+PACK = 4
+K_PASS = P * PACK
+PASSES = FEATURES // K_PASS
+PASS_WORDS = K_PASS // 2
+ROW_WORDS = FEATURES // 2
+N_TILE = 512
+GROUPS = HIDDEN // N_TILE
+ROW_BLOCKS = N_TILE // P
+CHUNKS = GATES * GROUPS * OPERANDS
+BANKS_PER_PASS = 2
+EPS = 1e-5
+
+RAW_BUFS = 5
+VECTOR_EVERY = 4
+
+FLOPS = 2 * P * GATES * HIDDEN * OPERANDS * FEATURES
+
+
+def words_onto_partitions(nc, psum, identity, blocks, dest, copy):
+    bank = psum.tile([P, 2, 2, P], F32, tag="bank")
+    for a in range(2):
+        for u in range(2):
+            nc.tensor.transpose(bank[:, a, u, :], blocks[a][:, u * P : (u + 1) * P], identity)
+    copy(
+        out=dest.rearrange("p (a r u) -> p a r u", a=2, u=2),
+        in_=bank[:].rearrange("p a u r -> p a r u"),
+    )
+
+
+def tile_layernormlstmcell_pa_kernel(
+    tc, x, h, Wi_w, Wi_b, Ui_w, lni_g, lni_b, Wc_w, Wc_b, Uc_w, lnc_g, lnc_b, out
+):
+    nc = tc.nc
+    weights = ((Wi_w, Ui_w), (Wc_w, Uc_w))
+    vector_rows = (Wi_b, Wc_b, lni_g, lni_b, lnc_g, lnc_b)
+    functions = (ACT.Sigmoid, ACT.Tanh)
+
+    with ExitStack() as ctx:
+        ctx.enter_context(tc.manual_schedule())
+        keep = ctx.enter_context(tc.tile_pool(name="keep", bufs=1))
+        raw_pool = ctx.enter_context(tc.tile_pool(name="raw", bufs=RAW_BUFS))
+        grouped_pool = ctx.enter_context(tc.tile_pool(name="grouped", bufs=4))
+        mx_pool = ctx.enter_context(tc.tile_pool(name="mx", bufs=3))
+        work_psum = ctx.enter_context(tc.psum_pool(name="work_psum", bufs=6))
+        acc_psum = ctx.enter_context(tc.psum_pool(name="acc_psum", bufs=2))
+
+        a_raw = []
+        for s, operand in enumerate((x, h)):
+            rows = keep.tile([P, FEATURES], BF16, name="a_raw%d" % s)
+            nc.sync.dma_start(out=rows[:], in_=operand)
+            a_raw.append(rows)
+
+        vectors = keep.tile([P, HIDDEN], BF16)
+        nc.vector.memset(vectors[:], 0.0)
+        for row, vector in enumerate(vector_rows):
+            nc.scalar.dma_start(out=vectors[row : row + 1, :], in_=vector.unsqueeze(0))
+
+        identity_words = keep.tile([P, P], F32)
+        make_identity(nc, identity_words[:])
+        identity_bf16 = keep.tile([P, P], BF16)
+        make_identity(nc, identity_bf16[:])
+        minus_half = keep.tile([P, 1], F32)
+        nc.vector.memset(minus_half[:], -0.5)
+
+        table_warmer = keep.tile([P, 1], F32)
+        nc.vector.memset(table_warmer[:], 0.0)
+        nc.scalar.activation(out=table_warmer[:], in_=table_warmer[:], func=ACT.Sigmoid)
+
+        a_codes = keep.tile([P, OPERANDS * PASSES * P], U32, align_bytes=64)
+        a_scales = keep.tile([P, OPERANDS * PASSES * P], U8, align_bytes=64)
+        for s in range(OPERANDS):
+            a_words = a_raw[s][:].bitcast(F32)
+            a_grouped = keep.tile([P, PASSES * P * PACK], BF16, align_bytes=64, name="a_grouped%d" % s)
+            a_grouped_words = a_grouped[:].bitcast(F32)
+            for pair in range(PASSES // 2):
+                first = 2 * pair * PASS_WORDS
+                words_onto_partitions(
+                    nc,
+                    work_psum,
+                    identity_words[:],
+                    [a_words[:, first + a * PASS_WORDS : first + (a + 1) * PASS_WORDS] for a in range(2)],
+                    a_grouped_words[:, first : first + 2 * PASS_WORDS],
+                    nc.vector.tensor_copy if pair % 2 else nc.scalar.copy,
+                )
+            a_cols = slice(s * PASSES * P, (s + 1) * PASSES * P)
+            nc.vector.quantize_mx(
+                out=a_codes[:, a_cols].bitcast(FP8X4), scales=a_scales[:, a_cols], in_=a_grouped[:]
+            )
+
+        def spread_row(dest, row, cols):
+            nc.tensor.matmul(
+                out=dest,
+                lhsT=identity_bf16[:, row : row + 1].to_broadcast([P, P]),
+                rhs=vectors[:, cols],
+                start=True,
+                stop=True,
+            )
+
+        bias = keep.tile([P, GATES, HIDDEN], BF16)
+        for gate in range(GATES):
+            for half in range(GROUPS // 2):
+                spread = work_psum.tile([P, 2, N_TILE], BF16, tag="bank")
+                for s in range(2):
+                    first = (2 * half + s) * N_TILE
+                    spread_row(spread[:, s, :], gate, slice(first, first + N_TILE))
+                nc.scalar.copy(
+                    out=bias[:, gate, 2 * half * N_TILE : 2 * (half + 1) * N_TILE],
+                    in_=spread[:].rearrange("p s n -> p (s n)"),
+                )
+
+        pre = [keep.tile([P, HIDDEN], F32, name="pre%d" % gate) for gate in range(GATES)]
+        stats = [keep.tile([P, GROUPS, 6], F32, name="stats%d" % gate) for gate in range(GATES)]
+        mean_var = [keep.tile([P, 2], F32, name="mean_var%d" % gate) for gate in range(GATES)]
+        var_eps = [keep.tile([P, 1], F32, name="var_eps%d" % gate) for gate in range(GATES)]
+        rstd = [keep.tile([P, 1], F32, name="rstd%d" % gate) for gate in range(GATES)]
+
+        w_grouped = {}
+        w_codes = {}
+        w_scales = {}
+        acc = {}
+
+        def place(chunk):
+            gate, rest = divmod(chunk, GROUPS * OPERANDS)
+            group, operand = divmod(rest, OPERANDS)
+            return gate, group, operand
+
+        def regroup(chunk):
+            gate, group, operand = place(chunk)
+            raw = raw_pool.tile([P, ROW_BLOCKS * FEATURES], BF16)
+            nc.sync.dma_start(
+                out=raw[:].rearrange("p (t k) -> p t k", t=ROW_BLOCKS),
+                in_=weights[gate][operand][group * N_TILE : (group + 1) * N_TILE, :].rearrange(
+                    "(t p) k -> p t k", p=P
+                ),
+            )
+            raw_words = raw[:].bitcast(F32)
+            codes = mx_pool.tile([P, PASSES * N_TILE], U32, align_bytes=64)
+            scales = mx_pool.tile([P, PASSES * N_TILE], U8, align_bytes=64)
+            w_codes[chunk] = codes
+            w_scales[chunk] = scales
+            for g in range(PASSES):
+                grouped = grouped_pool.tile([P, N_TILE * PACK], BF16, align_bytes=64)
+                w_grouped[chunk, g] = grouped
+                grouped_words = grouped[:].bitcast(F32)
+                for half in range(BANKS_PER_PASS):
+                    bank_index = g * BANKS_PER_PASS + half
+                    blocks = []
+                    for a in range(2):
+                        first = (2 * half + a) * ROW_WORDS + g * PASS_WORDS
+                        blocks.append(raw_words[:, first : first + PASS_WORDS])
+                    words_onto_partitions(
+                        nc,
+                        work_psum,
+                        identity_words[:],
+                        blocks,
+                        grouped_words[:, half * N_TILE : (half + 1) * N_TILE],
+                        nc.vector.tensor_copy if bank_index % VECTOR_EVERY == VECTOR_EVERY - 1 else nc.scalar.copy,
+                    )
+                if g > 0:
+                    quantise(chunk, g - 1)
+                elif chunk > 0:
+                    quantise(chunk - 1, PASSES - 1)
+
+        def quantise(chunk, g):
+            cols = slice(g * N_TILE, (g + 1) * N_TILE)
+            nc.vector.quantize_mx(
+                out=w_codes[chunk][:, cols].bitcast(FP8X4),
+                scales=w_scales[chunk][:, cols],
+                in_=w_grouped[chunk, g][:],
+            )
+
+        def multiply(chunk):
+            gate, group, operand = place(chunk)
+            if operand == 0:
+                bank = acc_psum.tile([P, N_TILE], F32, tag="acc")
+                acc[gate, group] = bank
+            for g in range(PASSES):
+                a_cols = slice((operand * PASSES + g) * P, (operand * PASSES + g + 1) * P)
+                w_cols = slice(g * N_TILE, (g + 1) * N_TILE)
+                nc.tensor.matmul_mx(
+                    out=acc[gate, group][:],
+                    lhsT=a_codes[:, a_cols].bitcast(FP8X4),
+                    lhsT_scale=a_scales[:, a_cols],
+                    rhs=w_codes[chunk][:, w_cols].bitcast(FP8X4),
+                    rhs_scale=w_scales[chunk][:, w_cols],
+                    start=(operand == 0 and g == 0),
+                    stop=(operand == OPERANDS - 1 and g == PASSES - 1),
+                )
+            if operand == OPERANDS - 1:
+                cols = slice(group * N_TILE, (group + 1) * N_TILE)
+                nc.vector.tensor_tensor(
+                    out=pre[gate][:, cols], in0=acc[gate, group][:], in1=bias[:, gate, cols], op=ALU.add
+                )
+                nc.vector.bn_stats(out=stats[gate][:, group, :], in_=pre[gate][:, cols])
+
+        def moments(gate):
+            nc.vector.bn_aggr(out=mean_var[gate][:], in_=stats[gate][:].rearrange("p g s -> p (g s)"))
+            nc.vector.tensor_scalar(
+                out=var_eps[gate][:], in0=mean_var[gate][:, 1:2], scalar1=EPS, scalar2=None, op0=ALU.add
+            )
+            nc.gpsimd.tensor_tensor(out=rstd[gate][:], in0=var_eps[gate][:], in1=minus_half[:], op=ALU.pow)
+
+        def activate(gate, group):
+            cols = slice(group * N_TILE, (group + 1) * N_TILE)
+            gain_shift = work_psum.tile([P, 2, N_TILE], BF16, tag="bank")
+            spread_row(gain_shift[:, 0, :], 2 + 2 * gate, cols)
+            spread_row(gain_shift[:, 1, :], 3 + 2 * gate, cols)
+            values = pre[gate][:, cols]
+            nc.vector.scalar_tensor_tensor(
+                out=values,
+                in0=values,
+                scalar=mean_var[gate][:, 0:1],
+                in1=gain_shift[:, 0, :],
+                op0=ALU.subtract,
+                op1=ALU.mult,
+            )
+            nc.vector.scalar_tensor_tensor(
+                out=values,
+                in0=values,
+                scalar=rstd[gate][:],
+                in1=gain_shift[:, 1, :],
+                op0=ALU.mult,
+                op1=ALU.add,
+            )
+            nc.scalar.activation(out=values, in_=values, func=functions[gate])
+
+        def product(group):
+            cols = slice(group * N_TILE, (group + 1) * N_TILE)
+            nc.vector.tensor_tensor(out=pre[1][:, cols], in0=pre[1][:, cols], in1=pre[0][:, cols], op=ALU.mult)
+            nc.sync.dma_start(out=out[:, cols], in_=pre[1][:, cols])
+
+        first_gate_chunks = GROUPS * OPERANDS
+        for chunk in range(CHUNKS):
+            regroup(chunk)
+            if chunk > 0:
+                multiply(chunk - 1)
+            if chunk == first_gate_chunks:
+                moments(0)
+            if first_gate_chunks < chunk <= first_gate_chunks + GROUPS:
+                activate(0, chunk - first_gate_chunks - 1)
+        quantise(CHUNKS - 1, PASSES - 1)
+        multiply(CHUNKS - 1)
+
+        moments(1)
+        for group in range(GROUPS + 1):
+            if group < GROUPS:
+                activate(1, group)
+            if group > 0:
+                product(group - 1)

@@ -21,15 +21,19 @@ K_PASS = P * PACK
 PASSES = FEATURES // K_PASS
 PASS_WORDS = K_PASS // 2
 ROW_WORDS = FEATURES // 2
-N_TILE = 512
+N_TILE = 2 * P
 GROUPS = HIDDEN // N_TILE
-ROW_BLOCKS = N_TILE // P
-CHUNKS = GATES * GROUPS * OPERANDS
-BANKS_PER_PASS = 2
+ROUNDS = GATES * GROUPS * OPERANDS
+BANK_WORDS = 512
+PIECE = 512
+PIECES = HIDDEN // PIECE
+STATS = 6
 EPS = 1e-5
 
-RAW_BUFS = 5
-VECTOR_EVERY = 4
+RAW_BUFS = 8
+MX_LAG = 2
+VECTOR_EVERY = 8
+VECTOR_BANK = 5
 
 FLOPS = 2 * P * GATES * HIDDEN * OPERANDS * FEATURES
 
@@ -58,7 +62,7 @@ def tile_layernormlstmcell_pa_kernel(
         keep = ctx.enter_context(tc.tile_pool(name="keep", bufs=1))
         raw_pool = ctx.enter_context(tc.tile_pool(name="raw", bufs=RAW_BUFS))
         grouped_pool = ctx.enter_context(tc.tile_pool(name="grouped", bufs=4))
-        mx_pool = ctx.enter_context(tc.tile_pool(name="mx", bufs=3))
+        mx_pool = ctx.enter_context(tc.tile_pool(name="mx", bufs=MX_LAG + 2))
         work_psum = ctx.enter_context(tc.psum_pool(name="work_psum", bufs=6))
         acc_psum = ctx.enter_context(tc.psum_pool(name="acc_psum", bufs=2))
 
@@ -97,7 +101,7 @@ def tile_layernormlstmcell_pa_kernel(
                     work_psum,
                     identity_words[:],
                     [a_words[:, first + a * PASS_WORDS : first + (a + 1) * PASS_WORDS] for a in range(2)],
-                    a_grouped_words[:, first : first + 2 * PASS_WORDS],
+                    a_grouped_words[:, first : first + BANK_WORDS],
                     nc.vector.tensor_copy if pair % 2 else nc.scalar.copy,
                 )
             a_cols = slice(s * PASSES * P, (s + 1) * PASSES * P)
@@ -115,80 +119,76 @@ def tile_layernormlstmcell_pa_kernel(
             )
 
         bias = keep.tile([P, GATES, HIDDEN], BF16)
-        for gate in range(GATES):
-            for half in range(GROUPS // 2):
-                spread = work_psum.tile([P, 2, N_TILE], BF16, tag="bank")
-                for s in range(2):
-                    first = (2 * half + s) * N_TILE
-                    spread_row(spread[:, s, :], gate, slice(first, first + N_TILE))
-                nc.scalar.copy(
-                    out=bias[:, gate, 2 * half * N_TILE : 2 * (half + 1) * N_TILE],
-                    in_=spread[:].rearrange("p s n -> p (s n)"),
-                )
+
+        def spread_bias(quarter):
+            gate, half = divmod(quarter, 2)
+            spread = work_psum.tile([P, 2, PIECE], BF16, tag="bank")
+            for s in range(2):
+                first = (2 * half + s) * PIECE
+                spread_row(spread[:, s, :], gate, slice(first, first + PIECE))
+            nc.scalar.copy(
+                out=bias[:, gate, 2 * half * PIECE : 2 * (half + 1) * PIECE],
+                in_=spread[:].rearrange("p s n -> p (s n)"),
+            )
 
         pre = [keep.tile([P, HIDDEN], F32, name="pre%d" % gate) for gate in range(GATES)]
-        stats = [keep.tile([P, GROUPS, 6], F32, name="stats%d" % gate) for gate in range(GATES)]
+        stats = [keep.tile([P, GROUPS, STATS], F32, name="stats%d" % gate) for gate in range(GATES)]
         mean_var = [keep.tile([P, 2], F32, name="mean_var%d" % gate) for gate in range(GATES)]
         var_eps = [keep.tile([P, 1], F32, name="var_eps%d" % gate) for gate in range(GATES)]
         rstd = [keep.tile([P, 1], F32, name="rstd%d" % gate) for gate in range(GATES)]
 
+        raw_words = {}
         w_grouped = {}
         w_codes = {}
         w_scales = {}
         acc = {}
+        gain_shift = {}
 
-        def place(chunk):
-            gate, rest = divmod(chunk, GROUPS * OPERANDS)
+        def place(r):
+            gate, rest = divmod(r, GROUPS * OPERANDS)
             group, operand = divmod(rest, OPERANDS)
             return gate, group, operand
 
-        def regroup(chunk):
-            gate, group, operand = place(chunk)
-            raw = raw_pool.tile([P, ROW_BLOCKS * FEATURES], BF16)
+        def load(r):
+            gate, group, operand = place(r)
+            raw = raw_pool.tile([P, 2 * FEATURES], BF16)
             nc.sync.dma_start(
-                out=raw[:].rearrange("p (t k) -> p t k", t=ROW_BLOCKS),
+                out=raw[:].rearrange("p (a k) -> p a k", a=2),
                 in_=weights[gate][operand][group * N_TILE : (group + 1) * N_TILE, :].rearrange(
-                    "(t p) k -> p t k", p=P
+                    "(a p) k -> p a k", p=P
                 ),
             )
-            raw_words = raw[:].bitcast(F32)
+            raw_words[r] = raw[:].bitcast(F32)
             codes = mx_pool.tile([P, PASSES * N_TILE], U32, align_bytes=64)
             scales = mx_pool.tile([P, PASSES * N_TILE], U8, align_bytes=64)
-            w_codes[chunk] = codes
-            w_scales[chunk] = scales
-            for g in range(PASSES):
-                grouped = grouped_pool.tile([P, N_TILE * PACK], BF16, align_bytes=64)
-                w_grouped[chunk, g] = grouped
-                grouped_words = grouped[:].bitcast(F32)
-                for half in range(BANKS_PER_PASS):
-                    bank_index = g * BANKS_PER_PASS + half
-                    blocks = []
-                    for a in range(2):
-                        first = (2 * half + a) * ROW_WORDS + g * PASS_WORDS
-                        blocks.append(raw_words[:, first : first + PASS_WORDS])
-                    words_onto_partitions(
-                        nc,
-                        work_psum,
-                        identity_words[:],
-                        blocks,
-                        grouped_words[:, half * N_TILE : (half + 1) * N_TILE],
-                        nc.vector.tensor_copy if bank_index % VECTOR_EVERY == VECTOR_EVERY - 1 else nc.scalar.copy,
-                    )
-                if g > 0:
-                    quantise(chunk, g - 1)
-                elif chunk > 0:
-                    quantise(chunk - 1, PASSES - 1)
+            w_codes[r] = codes
+            w_scales[r] = scales
 
-        def quantise(chunk, g):
-            cols = slice(g * N_TILE, (g + 1) * N_TILE)
+        def regroup(r, half):
+            grouped = grouped_pool.tile([P, 2 * N_TILE * PACK], BF16, align_bytes=64)
+            w_grouped[r, half] = grouped
+            grouped_words = grouped[:].bitcast(F32)
+            for s in range(2):
+                g = 2 * half + s
+                first = g * PASS_WORDS
+                on_vector = (r * PASSES + g) % VECTOR_EVERY == VECTOR_BANK
+                words_onto_partitions(
+                    nc,
+                    work_psum,
+                    identity_words[:],
+                    [raw_words[r][:, a * ROW_WORDS + first : a * ROW_WORDS + first + PASS_WORDS] for a in range(2)],
+                    grouped_words[:, s * BANK_WORDS : (s + 1) * BANK_WORDS],
+                    nc.vector.tensor_copy if on_vector else nc.scalar.copy,
+                )
+
+        def quantise(r, half):
+            cols = slice(2 * half * N_TILE, 2 * (half + 1) * N_TILE)
             nc.vector.quantize_mx(
-                out=w_codes[chunk][:, cols].bitcast(FP8X4),
-                scales=w_scales[chunk][:, cols],
-                in_=w_grouped[chunk, g][:],
+                out=w_codes[r][:, cols].bitcast(FP8X4), scales=w_scales[r][:, cols], in_=w_grouped[r, half][:]
             )
 
-        def multiply(chunk):
-            gate, group, operand = place(chunk)
+        def multiply(r):
+            gate, group, operand = place(r)
             if operand == 0:
                 bank = acc_psum.tile([P, N_TILE], F32, tag="acc")
                 acc[gate, group] = bank
@@ -199,8 +199,8 @@ def tile_layernormlstmcell_pa_kernel(
                     out=acc[gate, group][:],
                     lhsT=a_codes[:, a_cols].bitcast(FP8X4),
                     lhsT_scale=a_scales[:, a_cols],
-                    rhs=w_codes[chunk][:, w_cols].bitcast(FP8X4),
-                    rhs_scale=w_scales[chunk][:, w_cols],
+                    rhs=w_codes[r][:, w_cols].bitcast(FP8X4),
+                    rhs_scale=w_scales[r][:, w_cols],
                     start=(operand == 0 and g == 0),
                     stop=(operand == OPERANDS - 1 and g == PASSES - 1),
                 )
@@ -218,50 +218,65 @@ def tile_layernormlstmcell_pa_kernel(
             )
             nc.gpsimd.tensor_tensor(out=rstd[gate][:], in0=var_eps[gate][:], in1=minus_half[:], op=ALU.pow)
 
-        def activate(gate, group):
-            cols = slice(group * N_TILE, (group + 1) * N_TILE)
-            gain_shift = work_psum.tile([P, 2, N_TILE], BF16, tag="bank")
-            spread_row(gain_shift[:, 0, :], 2 + 2 * gate, cols)
-            spread_row(gain_shift[:, 1, :], 3 + 2 * gate, cols)
-            values = pre[gate][:, cols]
+        def centre(gate, piece):
+            cols = slice(piece * PIECE, (piece + 1) * PIECE)
+            spread = work_psum.tile([P, 2, PIECE], BF16, tag="bank")
+            gain_shift[gate, piece] = spread
+            spread_row(spread[:, 0, :], 2 + 2 * gate, cols)
+            spread_row(spread[:, 1, :], 3 + 2 * gate, cols)
             nc.vector.scalar_tensor_tensor(
-                out=values,
-                in0=values,
+                out=pre[gate][:, cols],
+                in0=pre[gate][:, cols],
                 scalar=mean_var[gate][:, 0:1],
-                in1=gain_shift[:, 0, :],
+                in1=spread[:, 0, :],
                 op0=ALU.subtract,
                 op1=ALU.mult,
             )
+
+        def activate(gate, piece):
+            cols = slice(piece * PIECE, (piece + 1) * PIECE)
             nc.vector.scalar_tensor_tensor(
-                out=values,
-                in0=values,
+                out=pre[gate][:, cols],
+                in0=pre[gate][:, cols],
                 scalar=rstd[gate][:],
-                in1=gain_shift[:, 1, :],
+                in1=gain_shift[gate, piece][:, 1, :],
                 op0=ALU.mult,
                 op1=ALU.add,
             )
-            nc.scalar.activation(out=values, in_=values, func=functions[gate])
+            nc.scalar.activation(out=pre[gate][:, cols], in_=pre[gate][:, cols], func=functions[gate])
 
-        def product(group):
-            cols = slice(group * N_TILE, (group + 1) * N_TILE)
+        def product(piece):
+            cols = slice(piece * PIECE, (piece + 1) * PIECE)
             nc.vector.tensor_tensor(out=pre[1][:, cols], in0=pre[1][:, cols], in1=pre[0][:, cols], op=ALU.mult)
             nc.sync.dma_start(out=out[:, cols], in_=pre[1][:, cols])
 
-        first_gate_chunks = GROUPS * OPERANDS
-        for chunk in range(CHUNKS):
-            regroup(chunk)
-            if chunk > 0:
-                multiply(chunk - 1)
-            if chunk == first_gate_chunks:
+        spread_bias(0)
+        for r in range(ROUNDS):
+            load(r)
+            regroup(r, 0)
+            if r > 0:
+                quantise(r - 1, 1)
+            regroup(r, 1)
+            quantise(r, 0)
+            if r + 1 < GATES * 2:
+                spread_bias(r + 1)
+            if r >= MX_LAG:
+                multiply(r - MX_LAG)
+            since_gate_0 = r - MX_LAG - (ROUNDS // GATES - 1)
+            if since_gate_0 == 0:
                 moments(0)
-            if first_gate_chunks < chunk <= first_gate_chunks + GROUPS:
-                activate(0, chunk - first_gate_chunks - 1)
-        quantise(CHUNKS - 1, PASSES - 1)
-        multiply(CHUNKS - 1)
+            if since_gate_0 > 0 and since_gate_0 % 2 == 1 and since_gate_0 // 2 < PIECES:
+                centre(0, since_gate_0 // 2)
+                activate(0, since_gate_0 // 2)
+        quantise(ROUNDS - 1, 1)
+        for r in range(ROUNDS - MX_LAG, ROUNDS):
+            multiply(r)
 
         moments(1)
-        for group in range(GROUPS + 1):
-            if group < GROUPS:
-                activate(1, group)
-            if group > 0:
-                product(group - 1)
+        for step in range(PIECES + 2):
+            if step < PIECES:
+                centre(1, step)
+            if 0 <= step - 1 < PIECES:
+                activate(1, step - 1)
+            if step - 2 >= 0:
+                product(step - 2)

@@ -32,6 +32,7 @@ EPS = 1e-5
 
 RAW_BUFS = 8
 MX_LAG = 2
+GAINS_AFTER_ROUND = 3
 VECTOR_EVERY = 8
 VECTOR_BANK = 5
 
@@ -74,8 +75,12 @@ def tile_layernormlstmcell_pa_kernel(
 
         vectors = keep.tile([P, HIDDEN], BF16)
         nc.vector.memset(vectors[:], 0.0)
-        for row, vector in enumerate(vector_rows):
-            nc.scalar.dma_start(out=vectors[row : row + 1, :], in_=vector.unsqueeze(0))
+
+        def load_vector_rows(first, last):
+            for row in range(first, last):
+                nc.sync.dma_start(out=vectors[row : row + 1, :], in_=vector_rows[row].unsqueeze(0))
+
+        load_vector_rows(0, GATES)
 
         identity_words = keep.tile([P, P], F32)
         make_identity(nc, identity_words[:])
@@ -153,9 +158,9 @@ def tile_layernormlstmcell_pa_kernel(
             gate, group, operand = place(r)
             raw = raw_pool.tile([P, 2 * FEATURES], BF16)
             nc.sync.dma_start(
-                out=raw[:].rearrange("p (a k) -> p a k", a=2),
+                out=raw[:],
                 in_=weights[gate][operand][group * N_TILE : (group + 1) * N_TILE, :].rearrange(
-                    "(a p) k -> p a k", p=P
+                    "(p a) k -> p (a k)", a=2
                 ),
             )
             raw_words[r] = raw[:].bitcast(F32)
@@ -207,7 +212,10 @@ def tile_layernormlstmcell_pa_kernel(
             if operand == OPERANDS - 1:
                 cols = slice(group * N_TILE, (group + 1) * N_TILE)
                 nc.vector.tensor_tensor(
-                    out=pre[gate][:, cols], in0=acc[gate, group][:], in1=bias[:, gate, cols], op=ALU.add
+                    out=pre[gate][:, cols].rearrange("p (r a) -> p r a", a=2),
+                    in0=acc[gate, group][:].rearrange("p (a r) -> p r a", a=2),
+                    in1=bias[:, gate, cols].rearrange("p (r a) -> p r a", a=2),
+                    op=ALU.add,
                 )
                 nc.vector.bn_stats(out=stats[gate][:, group, :], in_=pre[gate][:, cols])
 
@@ -253,6 +261,8 @@ def tile_layernormlstmcell_pa_kernel(
         spread_bias(0)
         for r in range(ROUNDS):
             load(r)
+            if r == GAINS_AFTER_ROUND:
+                load_vector_rows(GATES, len(vector_rows))
             regroup(r, 0)
             if r > 0:
                 quantise(r - 1, 1)

@@ -32,7 +32,6 @@ EPS = 1e-5
 
 RAW_BUFS = 8
 MX_LAG = 2
-GAINS_AFTER_ROUND = 3
 VECTOR_EVERY = 8
 VECTOR_BANK = 5
 
@@ -73,19 +72,15 @@ def tile_layernormlstmcell_pa_kernel(
             nc.sync.dma_start(out=rows[:], in_=operand)
             a_raw.append(rows)
 
-        vectors = keep.tile([P, HIDDEN], BF16)
-        nc.vector.memset(vectors[:], 0.0)
-
-        def load_vector_rows(first, last):
-            for row in range(first, last):
-                nc.sync.dma_start(out=vectors[row : row + 1, :], in_=vector_rows[row].unsqueeze(0))
-
-        load_vector_rows(0, GATES)
-
         identity_words = keep.tile([P, P], F32)
         make_identity(nc, identity_words[:])
         identity_bf16 = keep.tile([P, P], BF16)
         make_identity(nc, identity_bf16[:])
+
+        vectors = keep.tile([P, HIDDEN], BF16)
+        nc.vector.memset(vectors[:], 0.0)
+        for row, vector in enumerate(vector_rows):
+            nc.gpsimd.dma_start(out=vectors[row : row + 1, :], in_=vector.unsqueeze(0))
         minus_half = keep.tile([P, 1], F32)
         nc.vector.memset(minus_half[:], -0.5)
 
@@ -255,21 +250,19 @@ def tile_layernormlstmcell_pa_kernel(
 
         def product(piece):
             cols = slice(piece * PIECE, (piece + 1) * PIECE)
-            nc.vector.tensor_tensor(out=pre[1][:, cols], in0=pre[1][:, cols], in1=pre[0][:, cols], op=ALU.mult)
+            engine = nc.gpsimd if piece < PIECES // 2 else nc.vector
+            engine.tensor_tensor(out=pre[1][:, cols], in0=pre[1][:, cols], in1=pre[0][:, cols], op=ALU.mult)
             nc.sync.dma_start(out=out[:, cols], in_=pre[1][:, cols])
 
-        spread_bias(0)
         for r in range(ROUNDS):
             load(r)
-            if r == GAINS_AFTER_ROUND:
-                load_vector_rows(GATES, len(vector_rows))
             regroup(r, 0)
             if r > 0:
                 quantise(r - 1, 1)
             regroup(r, 1)
             quantise(r, 0)
-            if r + 1 < GATES * 2:
-                spread_bias(r + 1)
+            if r < GATES * 2:
+                spread_bias(r)
             if r >= MX_LAG:
                 multiply(r - MX_LAG)
             since_gate_0 = r - MX_LAG - (ROUNDS // GATES - 1)

from contextlib import ExitStack

import concourse.mybir as mybir
from concourse.masks import make_identity

F32 = mybir.dt.float32
BF16 = mybir.dt.bfloat16
U32 = mybir.dt.uint32
U8 = mybir.dt.uint8
FP8X4 = mybir.dt.float8_e4m3fn_x4
ALU = mybir.AluOpType
ACT = mybir.ActivationFunctionType

P = 128
FEATURES = 2048
HIDDEN = 2048
GATES = 2
OPERANDS = 2
PACK = 4
K_PASS = P * PACK
PASSES = FEATURES // K_PASS
PASS_WORDS = K_PASS // 2
ROW_WORDS = FEATURES // 2
N_TILE = 2 * P
GROUPS = HIDDEN // N_TILE
ROUNDS = GATES * GROUPS * OPERANDS
BANK_WORDS = 512
PIECE = 512
PIECES = HIDDEN // PIECE
STATS = 6
EPS = 1e-5

RAW_BUFS = 8
MX_LAG = 2
VECTOR_EVERY = 8
VECTOR_BANK = 5

FLOPS = 2 * P * GATES * HIDDEN * OPERANDS * FEATURES


def words_onto_partitions(nc, psum, identity, blocks, dest, copy):
    bank = psum.tile([P, 2, 2, P], F32, tag="bank")
    for a in range(2):
        for u in range(2):
            nc.tensor.transpose(bank[:, a, u, :], blocks[a][:, u * P : (u + 1) * P], identity)
    copy(
        out=dest.rearrange("p (a r u) -> p a r u", a=2, u=2),
        in_=bank[:].rearrange("p a u r -> p a r u"),
    )


def tile_layernormlstmcell_pa_kernel(
    tc, x, h, Wi_w, Wi_b, Ui_w, lni_g, lni_b, Wc_w, Wc_b, Uc_w, lnc_g, lnc_b, out
):
    nc = tc.nc
    weights = ((Wi_w, Ui_w), (Wc_w, Uc_w))
    vector_rows = (Wi_b, Wc_b, lni_g, lni_b, lnc_g, lnc_b)
    functions = (ACT.Sigmoid, ACT.Tanh)

    with ExitStack() as ctx:
        ctx.enter_context(tc.manual_schedule())
        keep = ctx.enter_context(tc.tile_pool(name="keep", bufs=1))
        raw_pool = ctx.enter_context(tc.tile_pool(name="raw", bufs=RAW_BUFS))
        grouped_pool = ctx.enter_context(tc.tile_pool(name="grouped", bufs=4))
        mx_pool = ctx.enter_context(tc.tile_pool(name="mx", bufs=MX_LAG + 2))
        work_psum = ctx.enter_context(tc.psum_pool(name="work_psum", bufs=6))
        acc_psum = ctx.enter_context(tc.psum_pool(name="acc_psum", bufs=2))

        a_raw = []
        for s, operand in enumerate((x, h)):
            rows = keep.tile([P, FEATURES], BF16, name="a_raw%d" % s)
            nc.sync.dma_start(out=rows[:], in_=operand)
            a_raw.append(rows)

        identity_words = keep.tile([P, P], F32)
        make_identity(nc, identity_words[:])
        identity_bf16 = keep.tile([P, P], BF16)
        make_identity(nc, identity_bf16[:])

        vectors = keep.tile([P, HIDDEN], BF16)
        nc.vector.memset(vectors[:], 0.0)
        for row, vector in enumerate(vector_rows):
            nc.gpsimd.dma_start(out=vectors[row : row + 1, :], in_=vector.unsqueeze(0))
        minus_half = keep.tile([P, 1], F32)
        nc.vector.memset(minus_half[:], -0.5)

        table_warmer = keep.tile([P, 1], F32)
        nc.vector.memset(table_warmer[:], 0.0)
        nc.scalar.activation(out=table_warmer[:], in_=table_warmer[:], func=ACT.Sigmoid)

        a_codes = keep.tile([P, OPERANDS * PASSES * P], U32, align_bytes=64)
        a_scales = keep.tile([P, OPERANDS * PASSES * P], U8, align_bytes=64)
        for s in range(OPERANDS):
            a_words = a_raw[s][:].bitcast(F32)
            a_grouped = keep.tile([P, PASSES * P * PACK], BF16, align_bytes=64, name="a_grouped%d" % s)
            a_grouped_words = a_grouped[:].bitcast(F32)
            for pair in range(PASSES // 2):
                first = 2 * pair * PASS_WORDS
                words_onto_partitions(
                    nc,
                    work_psum,
                    identity_words[:],
                    [a_words[:, first + a * PASS_WORDS : first + (a + 1) * PASS_WORDS] for a in range(2)],
                    a_grouped_words[:, first : first + BANK_WORDS],
                    nc.vector.tensor_copy if pair % 2 else nc.scalar.copy,
                )
            a_cols = slice(s * PASSES * P, (s + 1) * PASSES * P)
            nc.vector.quantize_mx(
                out=a_codes[:, a_cols].bitcast(FP8X4), scales=a_scales[:, a_cols], in_=a_grouped[:]
            )

        def spread_row(dest, row, cols):
            nc.tensor.matmul(
                out=dest,
                lhsT=identity_bf16[:, row : row + 1].to_broadcast([P, P]),
                rhs=vectors[:, cols],
                start=True,
                stop=True,
            )

        bias = keep.tile([P, GATES, HIDDEN], BF16)

        def spread_bias(quarter):
            gate, half = divmod(quarter, 2)
            spread = work_psum.tile([P, 2, PIECE], BF16, tag="bank")
            for s in range(2):
                first = (2 * half + s) * PIECE
                spread_row(spread[:, s, :], gate, slice(first, first + PIECE))
            nc.scalar.copy(
                out=bias[:, gate, 2 * half * PIECE : 2 * (half + 1) * PIECE],
                in_=spread[:].rearrange("p s n -> p (s n)"),
            )

        pre = [keep.tile([P, HIDDEN], F32, name="pre%d" % gate) for gate in range(GATES)]
        stats = [keep.tile([P, GROUPS, STATS], F32, name="stats%d" % gate) for gate in range(GATES)]
        mean_var = [keep.tile([P, 2], F32, name="mean_var%d" % gate) for gate in range(GATES)]
        var_eps = [keep.tile([P, 1], F32, name="var_eps%d" % gate) for gate in range(GATES)]
        rstd = [keep.tile([P, 1], F32, name="rstd%d" % gate) for gate in range(GATES)]

        raw_words = {}
        w_grouped = {}
        w_codes = {}
        w_scales = {}
        acc = {}
        gain_shift = {}

        def place(r):
            gate, rest = divmod(r, GROUPS * OPERANDS)
            group, operand = divmod(rest, OPERANDS)
            return gate, group, operand

        def load(r):
            gate, group, operand = place(r)
            raw = raw_pool.tile([P, 2 * FEATURES], BF16)
            nc.sync.dma_start(
                out=raw[:],
                in_=weights[gate][operand][group * N_TILE : (group + 1) * N_TILE, :].rearrange(
                    "(p a) k -> p (a k)", a=2
                ),
            )
            raw_words[r] = raw[:].bitcast(F32)
            codes = mx_pool.tile([P, PASSES * N_TILE], U32, align_bytes=64)
            scales = mx_pool.tile([P, PASSES * N_TILE], U8, align_bytes=64)
            w_codes[r] = codes
            w_scales[r] = scales

        def regroup(r, half):
            grouped = grouped_pool.tile([P, 2 * N_TILE * PACK], BF16, align_bytes=64)
            w_grouped[r, half] = grouped
            grouped_words = grouped[:].bitcast(F32)
            for s in range(2):
                g = 2 * half + s
                first = g * PASS_WORDS
                on_vector = (r * PASSES + g) % VECTOR_EVERY == VECTOR_BANK
                words_onto_partitions(
                    nc,
                    work_psum,
                    identity_words[:],
                    [raw_words[r][:, a * ROW_WORDS + first : a * ROW_WORDS + first + PASS_WORDS] for a in range(2)],
                    grouped_words[:, s * BANK_WORDS : (s + 1) * BANK_WORDS],
                    nc.vector.tensor_copy if on_vector else nc.scalar.copy,
                )

        def quantise(r, half):
            cols = slice(2 * half * N_TILE, 2 * (half + 1) * N_TILE)
            nc.vector.quantize_mx(
                out=w_codes[r][:, cols].bitcast(FP8X4), scales=w_scales[r][:, cols], in_=w_grouped[r, half][:]
            )

        def multiply(r):
            gate, group, operand = place(r)
            if operand == 0:
                bank = acc_psum.tile([P, N_TILE], F32, tag="acc")
                acc[gate, group] = bank
            for g in range(PASSES):
                a_cols = slice((operand * PASSES + g) * P, (operand * PASSES + g + 1) * P)
                w_cols = slice(g * N_TILE, (g + 1) * N_TILE)
                nc.tensor.matmul_mx(
                    out=acc[gate, group][:],
                    lhsT=a_codes[:, a_cols].bitcast(FP8X4),
                    lhsT_scale=a_scales[:, a_cols],
                    rhs=w_codes[r][:, w_cols].bitcast(FP8X4),
                    rhs_scale=w_scales[r][:, w_cols],
                    start=(operand == 0 and g == 0),
                    stop=(operand == OPERANDS - 1 and g == PASSES - 1),
                )
            if operand == OPERANDS - 1:
                cols = slice(group * N_TILE, (group + 1) * N_TILE)
                nc.vector.tensor_tensor(
                    out=pre[gate][:, cols].rearrange("p (r a) -> p r a", a=2),
                    in0=acc[gate, group][:].rearrange("p (a r) -> p r a", a=2),
                    in1=bias[:, gate, cols].rearrange("p (r a) -> p r a", a=2),
                    op=ALU.add,
                )
                nc.vector.bn_stats(out=stats[gate][:, group, :], in_=pre[gate][:, cols])

        def moments(gate):
            nc.vector.bn_aggr(out=mean_var[gate][:], in_=stats[gate][:].rearrange("p g s -> p (g s)"))
            nc.vector.tensor_scalar(
                out=var_eps[gate][:], in0=mean_var[gate][:, 1:2], scalar1=EPS, scalar2=None, op0=ALU.add
            )
            nc.gpsimd.tensor_tensor(out=rstd[gate][:], in0=var_eps[gate][:], in1=minus_half[:], op=ALU.pow)

        def centre(gate, piece):
            cols = slice(piece * PIECE, (piece + 1) * PIECE)
            spread = work_psum.tile([P, 2, PIECE], BF16, tag="bank")
            gain_shift[gate, piece] = spread
            spread_row(spread[:, 0, :], 2 + 2 * gate, cols)
            spread_row(spread[:, 1, :], 3 + 2 * gate, cols)
            nc.vector.scalar_tensor_tensor(
                out=pre[gate][:, cols],
                in0=pre[gate][:, cols],
                scalar=mean_var[gate][:, 0:1],
                in1=spread[:, 0, :],
                op0=ALU.subtract,
                op1=ALU.mult,
            )

        def activate(gate, piece):
            cols = slice(piece * PIECE, (piece + 1) * PIECE)
            nc.vector.scalar_tensor_tensor(
                out=pre[gate][:, cols],
                in0=pre[gate][:, cols],
                scalar=rstd[gate][:],
                in1=gain_shift[gate, piece][:, 1, :],
                op0=ALU.mult,
                op1=ALU.add,
            )
            nc.scalar.activation(out=pre[gate][:, cols], in_=pre[gate][:, cols], func=functions[gate])

        def product(piece):
            cols = slice(piece * PIECE, (piece + 1) * PIECE)
            engine = nc.gpsimd if piece < PIECES // 2 else nc.vector
            engine.tensor_tensor(out=pre[1][:, cols], in0=pre[1][:, cols], in1=pre[0][:, cols], op=ALU.mult)
            nc.sync.dma_start(out=out[:, cols], in_=pre[1][:, cols])

        for r in range(ROUNDS):
            load(r)
            regroup(r, 0)
            if r > 0:
                quantise(r - 1, 1)
            regroup(r, 1)
            quantise(r, 0)
            if r < GATES * 2:
                spread_bias(r)
            if r >= MX_LAG:
                multiply(r - MX_LAG)
            since_gate_0 = r - MX_LAG - (ROUNDS // GATES - 1)
            if since_gate_0 == 0:
                moments(0)
            if since_gate_0 > 0 and since_gate_0 % 2 == 1 and since_gate_0 // 2 < PIECES:
                centre(0, since_gate_0 // 2)
                activate(0, since_gate_0 // 2)
        quantise(ROUNDS - 1, 1)
        for r in range(ROUNDS - MX_LAG, ROUNDS):
            multiply(r)

        moments(1)
        for step in range(PIECES + 2):
            if step < PIECES:
                centre(1, step)
            if 0 <= step - 1 < PIECES:
                activate(1, step - 1)
            if step - 2 >= 0:
                product(step - 2)
